import numpy as np
import ml_dtypes


def mxq(x, axis, fmt="e4m3"):
    dtype, down = {"e4m3": (ml_dtypes.float8_e4m3fn, 7), "e5m2": (ml_dtypes.float8_e5m2, 14)}[fmt]
    v = np.moveaxis(np.asarray(x, np.float32).astype(ml_dtypes.bfloat16).astype(np.float64), axis, -1)
    blocks = v.reshape(v.shape[:-1] + (-1, 32))
    amax = np.abs(blocks).max(-1, keepdims=True)
    byte = np.maximum(np.where(amax > 0, np.frexp(amax)[1] - 1 + 127, 0) - down, 1)
    scale = np.exp2(byte - 127.0)
    codes = (blocks / scale).astype(np.float32).astype(dtype).astype(np.float64)
    return np.moveaxis((codes * scale).reshape(v.shape), -1, axis)


WIDE = False


def mx_kscale(k):
    if not WIDE:
        return np.ones(k)
    levels = np.array([20, -20, 10, -10, 0])
    a = np.random.permutation(np.resize(levels, k // 512 * 4)).reshape(k // 512, 4)
    idx = np.arange(k)
    return np.exp2(a[idx // 512, idx % 128 // 32])


BF16 = ml_dtypes.bfloat16


def bf(x):
    return np.asarray(x, np.float32).astype(BF16)


def f64(x):
    return np.asarray(x).astype(np.float64)


B, EN_MID, DE_MID = 3072, 1024, 512
K1 = EN_MID // 2
K2 = DE_MID // 2


def setup_inputs():
    h = mx_kscale(DE_MID)[:K2]
    u = np.concatenate([h, h])
    in_data = bf(np.random.standard_normal((B, K1, 2)).reshape(B, EN_MID))
    W0 = bf(np.random.standard_normal((DE_MID, K1)) / np.sqrt(K1))
    bias = bf(np.random.standard_normal(DE_MID) * 0.25)
    g = np.random.standard_normal((B, K2, 2)) * np.exp2(np.random.randint(-12, 1, (B, 1, 1))) * 64.0
    g = g * h[None, :, None]
    z = f64(in_data)[:, 1::2] @ f64(W0).T + f64(bias)
    return {"in_data": in_data,
            "W": bf(f64(W0) / u[:, None]),
            "bias": bias,
            "z": np.asarray(z, np.float32),
            "grad_out": bf(g.reshape(B, DE_MID, 1))}


def reference(in_data, W, bias, z, grad_out):
    zf = f64(z)
    gr = f64(grad_out)[:, 0::2, 0]
    dz = np.concatenate([gr, -gr], axis=1) * (zf > 0.0)
    dx = mxq(dz, 1, "e5m2") @ mxq(f64(W), 0, "e4m3")
    res = np.stack([np.zeros_like(dx), dx], axis=2)
    return res.reshape(zf.shape[0], EN_MID)

@@ -1,0 +1,141 @@
+from contextlib import ExitStack
+
+import concourse.masks as masks
+import concourse.mybir as mybir
+
+F32 = mybir.dt.float32
+BF16 = mybir.dt.bfloat16
+U32 = mybir.dt.uint32
+U8 = mybir.dt.uint8
+E4M3_X4 = mybir.dt.float8_e4m3fn_x4
+E5M2_X4 = mybir.dt.float8_e5m2_x4
+ALU = mybir.AluOpType
+ACT = mybir.ActivationFunctionType
+
+P = 128
+PACK = 4
+TOKENS = 3072
+HIDDEN = P * PACK
+HALF = HIDDEN // 2
+FEATURES = 512
+TILES = TOKENS // P
+CHUNK = 4
+CHUNKS = TILES // CHUNK
+BANK_TILES = 2
+
+FLOPS = 2 * TOKENS * HIDDEN * FEATURES
+BYTES = TOKENS * HIDDEN * 4 + TOKENS * HALF * 2 + HIDDEN * FEATURES * 2 + TOKENS * 2 * FEATURES * 4
+
+
+def tile_middlelayer_t_v_kernel(tc, in_data, W, bias, z, grad_out, out):
+    nc = tc.nc
+    z_view = z.rearrange("(p t) k -> p t k", t=TILES)
+    g_view = grad_out.rearrange("(p t) k o -> p t (k o)", t=TILES)
+    out_view = out.rearrange("(p t) n -> p t n", t=TILES)
+
+    with ExitStack() as ctx:
+        keep = ctx.enter_context(tc.tile_pool(name="keep", bufs=1))
+        loads = ctx.enter_context(tc.tile_pool(name="loads", bufs=CHUNKS))
+        work = ctx.enter_context(tc.tile_pool(name="work", bufs=3))
+        stores = ctx.enter_context(tc.tile_pool(name="stores", bufs=4))
+        psum_t = ctx.enter_context(tc.psum_pool(name="psum_t", bufs=4))
+        psum_mm = ctx.enter_context(tc.psum_pool(name="psum_mm", bufs=4))
+
+        w_rows = keep.tile([P, PACK, FEATURES], BF16)
+        nc.sync.dma_start(out=w_rows[:], in_=W.rearrange("(p j) n -> p j n", j=PACK))
+        z_chunks = []
+        g_chunks = []
+        for c in range(CHUNKS):
+            tiles = slice(c * CHUNK, (c + 1) * CHUNK)
+            z_chunk = loads.tile([P, CHUNK, HIDDEN], F32)
+            nc.sync.dma_start(out=z_chunk[:], in_=z_view[:, tiles, :])
+            g_chunk = loads.tile([P, CHUNK, HIDDEN], BF16)
+            nc.sync.dma_start(out=g_chunk[:], in_=g_view[:, tiles, :])
+            z_chunks.append(z_chunk)
+            g_chunks.append(g_chunk)
+
+        identity = keep.tile([P, P], F32)
+        masks.make_identity(nc, identity[:])
+        sign = keep.tile([P, 1], F32)
+        nc.vector.memset(sign[0 : P // 2, :], 1.0)
+        nc.vector.memset(sign[P // 2 : P, :], -1.0)
+        stages = []
+        for i in range(2):
+            stage = keep.tile([P, 2, CHUNK * FEATURES], F32, name="stage%d" % i)
+            nc.vector.memset(stage[:, 0, :], 0.0)
+            stages.append(stage)
+
+        w_grouped = keep.tile([P, FEATURES, PACK], BF16, align_bytes=64)
+        nc.vector.tensor_copy(out=w_grouped[:], in_=w_rows[:].rearrange("p j n -> p n j"))
+        w_codes = keep.tile([P, FEATURES], U32, align_bytes=64)
+        w_scales = keep.tile([P, FEATURES], U8, align_bytes=64)
+        nc.vector.quantize_mx(
+            out=w_codes[:].bitcast(E4M3_X4),
+            scales=w_scales[:],
+            in_=w_grouped[:].rearrange("p n j -> p (n j)"),
+        )
+
+        for c in range(CHUNKS):
+            tiles = slice(c * CHUNK, (c + 1) * CHUNK)
+            z_chunk = z_chunks[c]
+            g_chunk = g_chunks[c]
+
+            masked = work.tile([P, CHUNK, HIDDEN], BF16)
+            for i in range(CHUNK):
+                g_even = g_chunk[:, i, :].rearrange("p (j s) -> p s j", s=2)[:, 0:1, :]
+                nc.vector.scalar_tensor_tensor(
+                    out=masked[:, i, :].rearrange("p (h j) -> p h j", h=2),
+                    in0=z_chunk[:, i, :].rearrange("p (h j) -> p h j", h=2),
+                    scalar=0.0,
+                    in1=g_even.to_broadcast([P, 2, HALF]),
+                    op0=ALU.is_gt,
+                    op1=ALU.mult,
+                )
+
+            grouped = work.tile([P, CHUNK * P, PACK], BF16, align_bytes=64)
+            for b in range(CHUNK // BANK_TILES):
+                bank = psum_t.tile([P, 2, BANK_TILES * P], F32)
+                for i in range(BANK_TILES):
+                    words = masked[:, b * BANK_TILES + i, :].bitcast(F32)
+                    words = words.rearrange("p (q u) -> p u q", u=2)
+                    for u in range(2):
+                        nc.tensor.transpose(
+                            bank[:, u, i * P : (i + 1) * P], words[:, u, :], identity[:]
+                        )
+                tokens = slice(b * BANK_TILES * P, (b + 1) * BANK_TILES * P)
+                nc.scalar.activation(
+                    out=grouped[:, tokens, :].rearrange("p r (u e) -> p r u e", e=2),
+                    in_=bank[:].bitcast(BF16).rearrange("p u (r e) -> p r u e", e=2),
+                    func=ACT.Copy,
+                    scale=sign[:, 0:1],
+                )
+
+            dz_codes = work.tile([P, CHUNK * P], U32, align_bytes=64)
+            dz_scales = work.tile([P, CHUNK * P], U8, align_bytes=64)
+            nc.vector.quantize_mx(
+                out=dz_codes[:].bitcast(E5M2_X4),
+                scales=dz_scales[:],
+                in_=grouped[:].rearrange("p r t -> p (r t)"),
+            )
+
+            stage = stages[c % 2]
+            for i in range(CHUNK):
+                tokens = slice(i * P, (i + 1) * P)
+                acc = psum_mm.tile([P, FEATURES], F32)
+                nc.tensor.matmul_mx(
+                    out=acc[:],
+                    lhsT=dz_codes[:, tokens].bitcast(E5M2_X4),
+                    lhsT_scale=dz_scales[:, tokens],
+                    rhs=w_codes[:].bitcast(E4M3_X4),
+                    rhs_scale=w_scales[:],
+                    start=True,
+                    stop=True,
+                )
+                nc.scalar.copy(out=stage[:, 1, i * FEATURES : (i + 1) * FEATURES], in_=acc[:])
+
+            out_chunk = stores.tile([P, CHUNK * FEATURES, 2], F32)
+            nc.vector.tensor_copy(out=out_chunk[:], in_=stage[:].rearrange("p e m -> p m e"))
+            nc.sync.dma_start(
+                out=out_view[:, tiles, :],
+                in_=out_chunk[:].rearrange("p (i n) e -> p i (n e)", i=CHUNK),
+            )

@@ -19,9 +19,9 @@ HIDDEN = P * PACK
 HALF = HIDDEN // 2
 FEATURES = 512
 TILES = TOKENS // P
-CHUNK = 4
-CHUNKS = TILES // CHUNK
-BANK_TILES = 2
+GROUP = 2
+GROUPS = TILES // GROUP
+LOAD_MAX = 8
 
 FLOPS = 2 * TOKENS * HIDDEN * FEATURES
 BYTES = TOKENS * HIDDEN * 4 + TOKENS * HALF * 2 + HIDDEN * FEATURES * 2 + TOKENS * 2 * FEATURES * 4
@@ -35,24 +35,22 @@ def tile_middlelayer_t_v_kernel(tc, in_data, W, bias, z, grad_out, out):
 
     with ExitStack() as ctx:
         keep = ctx.enter_context(tc.tile_pool(name="keep", bufs=1))
-        loads = ctx.enter_context(tc.tile_pool(name="loads", bufs=CHUNKS))
         work = ctx.enter_context(tc.tile_pool(name="work", bufs=3))
-        stores = ctx.enter_context(tc.tile_pool(name="stores", bufs=4))
+        stores = ctx.enter_context(tc.tile_pool(name="stores", bufs=8))
         psum_t = ctx.enter_context(tc.psum_pool(name="psum_t", bufs=4))
         psum_mm = ctx.enter_context(tc.psum_pool(name="psum_mm", bufs=4))
 
         w_rows = keep.tile([P, PACK, FEATURES], BF16)
         nc.sync.dma_start(out=w_rows[:], in_=W.rearrange("(p j) n -> p j n", j=PACK))
-        z_chunks = []
-        g_chunks = []
-        for c in range(CHUNKS):
-            tiles = slice(c * CHUNK, (c + 1) * CHUNK)
-            z_chunk = loads.tile([P, CHUNK, HIDDEN], F32)
-            nc.sync.dma_start(out=z_chunk[:], in_=z_view[:, tiles, :])
-            g_chunk = loads.tile([P, CHUNK, HIDDEN], BF16)
-            nc.sync.dma_start(out=g_chunk[:], in_=g_view[:, tiles, :])
-            z_chunks.append(z_chunk)
-            g_chunks.append(g_chunk)
+        z_sb = keep.tile([P, TILES, HIDDEN], F32)
+        g_sb = keep.tile([P, TILES, HIDDEN], BF16)
+        loaded = 0
+        while loaded < TILES:
+            count = min(max(loaded, GROUP), LOAD_MAX)
+            tiles = slice(loaded, loaded + count)
+            nc.sync.dma_start(out=z_sb[:, tiles, :], in_=z_view[:, tiles, :])
+            nc.sync.dma_start(out=g_sb[:, tiles, :], in_=g_view[:, tiles, :])
+            loaded += count
 
         identity = keep.tile([P, P], F32)
         masks.make_identity(nc, identity[:])
@@ -60,8 +58,8 @@ def tile_middlelayer_t_v_kernel(tc, in_data, W, bias, z, grad_out, out):
         nc.vector.memset(sign[0 : P // 2, :], 1.0)
         nc.vector.memset(sign[P // 2 : P, :], -1.0)
         stages = []
-        for i in range(2):
-            stage = keep.tile([P, 2, CHUNK * FEATURES], F32, name="stage%d" % i)
+        for i in range(3):
+            stage = keep.tile([P, 2, GROUP * FEATURES], F32, name="stage%d" % i)
             nc.vector.memset(stage[:, 0, :], 0.0)
             stages.append(stage)
 
@@ -75,51 +73,45 @@ def tile_middlelayer_t_v_kernel(tc, in_data, W, bias, z, grad_out, out):
             in_=w_grouped[:].rearrange("p n j -> p (n j)"),
         )
 
-        for c in range(CHUNKS):
-            tiles = slice(c * CHUNK, (c + 1) * CHUNK)
-            z_chunk = z_chunks[c]
-            g_chunk = g_chunks[c]
+        for g in range(GROUPS):
+            tiles = slice(g * GROUP, (g + 1) * GROUP)
 
-            masked = work.tile([P, CHUNK, HIDDEN], BF16)
-            for i in range(CHUNK):
-                g_even = g_chunk[:, i, :].rearrange("p (j s) -> p s j", s=2)[:, 0:1, :]
+            masked = work.tile([P, GROUP, HIDDEN], BF16)
+            for i in range(GROUP):
+                t = g * GROUP + i
+                g_even = g_sb[:, t, :].rearrange("p (j s) -> p s j", s=2)[:, 0:1, :]
                 nc.vector.scalar_tensor_tensor(
                     out=masked[:, i, :].rearrange("p (h j) -> p h j", h=2),
-                    in0=z_chunk[:, i, :].rearrange("p (h j) -> p h j", h=2),
+                    in0=z_sb[:, t, :].rearrange("p (h j) -> p h j", h=2),
                     scalar=0.0,
                     in1=g_even.to_broadcast([P, 2, HALF]),
                     op0=ALU.is_gt,
                     op1=ALU.mult,
                 )
 
-            grouped = work.tile([P, CHUNK * P, PACK], BF16, align_bytes=64)
-            for b in range(CHUNK // BANK_TILES):
-                bank = psum_t.tile([P, 2, BANK_TILES * P], F32)
-                for i in range(BANK_TILES):
-                    words = masked[:, b * BANK_TILES + i, :].bitcast(F32)
-                    words = words.rearrange("p (q u) -> p u q", u=2)
-                    for u in range(2):
-                        nc.tensor.transpose(
-                            bank[:, u, i * P : (i + 1) * P], words[:, u, :], identity[:]
-                        )
-                tokens = slice(b * BANK_TILES * P, (b + 1) * BANK_TILES * P)
-                nc.scalar.activation(
-                    out=grouped[:, tokens, :].rearrange("p r (u e) -> p r u e", e=2),
-                    in_=bank[:].bitcast(BF16).rearrange("p u (r e) -> p r u e", e=2),
-                    func=ACT.Copy,
-                    scale=sign[:, 0:1],
-                )
+            bank = psum_t.tile([P, 2, GROUP * P], F32)
+            for i in range(GROUP):
+                words = masked[:, i, :].bitcast(F32).rearrange("p (q u) -> p u q", u=2)
+                for u in range(2):
+                    nc.tensor.transpose(bank[:, u, i * P : (i + 1) * P], words[:, u, :], identity[:])
+            grouped = work.tile([P, GROUP * P, PACK], BF16, align_bytes=64)
+            nc.scalar.activation(
+                out=grouped[:].rearrange("p r (u e) -> p r u e", e=2),
+                in_=bank[:].bitcast(BF16).rearrange("p u (r e) -> p r u e", e=2),
+                func=ACT.Copy,
+                scale=sign[:, 0:1],
+            )
 
-            dz_codes = work.tile([P, CHUNK * P], U32, align_bytes=64)
-            dz_scales = work.tile([P, CHUNK * P], U8, align_bytes=64)
+            dz_codes = work.tile([P, GROUP * P], U32, align_bytes=64)
+            dz_scales = work.tile([P, GROUP * P], U8, align_bytes=64)
             nc.vector.quantize_mx(
                 out=dz_codes[:].bitcast(E5M2_X4),
                 scales=dz_scales[:],
                 in_=grouped[:].rearrange("p r t -> p (r t)"),
             )
 
-            stage = stages[c % 2]
-            for i in range(CHUNK):
+            stage = stages[g % 3]
+            for i in range(GROUP):
                 tokens = slice(i * P, (i + 1) * P)
                 acc = psum_mm.tile([P, FEATURES], F32)
                 nc.tensor.matmul_mx(
@@ -133,9 +125,9 @@ def tile_middlelayer_t_v_kernel(tc, in_data, W, bias, z, grad_out, out):
                 )
                 nc.scalar.copy(out=stage[:, 1, i * FEATURES : (i + 1) * FEATURES], in_=acc[:])
 
-            out_chunk = stores.tile([P, CHUNK * FEATURES, 2], F32)
-            nc.vector.tensor_copy(out=out_chunk[:], in_=stage[:].rearrange("p e m -> p m e"))
+            out_group = stores.tile([P, GROUP * FEATURES, 2], F32)
+            nc.vector.tensor_copy(out=out_group[:], in_=stage[:].rearrange("p e m -> p m e"))
             nc.sync.dma_start(
                 out=out_view[:, tiles, :],
-                in_=out_chunk[:].rearrange("p (i n) e -> p i (n e)", i=CHUNK),
+                in_=out_group[:].rearrange("p (i n) e -> p i (n e)", i=GROUP),
             )

@@ -18,6 +18,8 @@ TOKENS = 3072
 HIDDEN = P * PACK
 HALF = HIDDEN // 2
 FEATURES = 512
+OUT_COLS = 2 * FEATURES
+BANK = 512
 TILES = TOKENS // P
 GROUP = 2
 GROUPS = TILES // GROUP
@@ -36,14 +38,15 @@ def tile_middlelayer_t_v_kernel(tc, in_data, W, bias, z, grad_out, out):
     with ExitStack() as ctx:
         keep = ctx.enter_context(tc.tile_pool(name="keep", bufs=1))
         work = ctx.enter_context(tc.tile_pool(name="work", bufs=3))
-        stores = ctx.enter_context(tc.tile_pool(name="stores", bufs=8))
-        psum_t = ctx.enter_context(tc.psum_pool(name="psum_t", bufs=4))
-        psum_mm = ctx.enter_context(tc.psum_pool(name="psum_mm", bufs=4))
+        psum_t = ctx.enter_context(tc.psum_pool(name="psum_t", bufs=2))
+        psum_mm = ctx.enter_context(tc.psum_pool(name="psum_mm", bufs=6))
+        ctx.enter_context(tc.manual_schedule())
 
         w_rows = keep.tile([P, PACK, FEATURES], BF16)
         nc.sync.dma_start(out=w_rows[:], in_=W.rearrange("(p j) n -> p j n", j=PACK))
         z_sb = keep.tile([P, TILES, HIDDEN], F32)
         g_sb = keep.tile([P, TILES, HIDDEN], BF16)
+        out_sb = keep.tile([P, TILES, OUT_COLS], F32)
         loaded = 0
         while loaded < TILES:
             count = min(max(loaded, GROUP), LOAD_MAX)
@@ -57,25 +60,20 @@ def tile_middlelayer_t_v_kernel(tc, in_data, W, bias, z, grad_out, out):
         sign = keep.tile([P, 1], F32)
         nc.vector.memset(sign[0 : P // 2, :], 1.0)
         nc.vector.memset(sign[P // 2 : P, :], -1.0)
-        stages = []
-        for i in range(3):
-            stage = keep.tile([P, 2, GROUP * FEATURES], F32, name="stage%d" % i)
-            nc.vector.memset(stage[:, 0, :], 0.0)
-            stages.append(stage)
 
-        w_grouped = keep.tile([P, FEATURES, PACK], BF16, align_bytes=64)
-        nc.vector.tensor_copy(out=w_grouped[:], in_=w_rows[:].rearrange("p j n -> p n j"))
-        w_codes = keep.tile([P, FEATURES], U32, align_bytes=64)
-        w_scales = keep.tile([P, FEATURES], U8, align_bytes=64)
-        nc.vector.quantize_mx(
-            out=w_codes[:].bitcast(E4M3_X4),
-            scales=w_scales[:],
-            in_=w_grouped[:].rearrange("p n j -> p (n j)"),
+        w_grouped = keep.tile([P, OUT_COLS, PACK], BF16, align_bytes=64)
+        w_pairs = w_grouped[:].rearrange("p (n e) j -> p n e j", e=2)
+        nc.vector.memset(w_pairs[:, :, 0, :], 0.0)
+        nc.scalar.activation(
+            out=w_pairs[:, :, 1, :],
+            in_=w_rows[:].rearrange("p j n -> p n j"),
+            func=ACT.Copy,
+            scale=sign[:, 0:1],
         )
+        w_codes = keep.tile([P, OUT_COLS], U32, align_bytes=64)
+        w_scales = keep.tile([P, OUT_COLS], U8, align_bytes=64)
 
-        for g in range(GROUPS):
-            tiles = slice(g * GROUP, (g + 1) * GROUP)
-
+        def mask(g):
             masked = work.tile([P, GROUP, HIDDEN], BF16)
             for i in range(GROUP):
                 t = g * GROUP + i
@@ -88,20 +86,19 @@ def tile_middlelayer_t_v_kernel(tc, in_data, W, bias, z, grad_out, out):
                     op0=ALU.is_gt,
                     op1=ALU.mult,
                 )
+            return masked
 
+        def flip(masked):
             bank = psum_t.tile([P, 2, GROUP * P], F32)
             for i in range(GROUP):
                 words = masked[:, i, :].bitcast(F32).rearrange("p (q u) -> p u q", u=2)
                 for u in range(2):
                     nc.tensor.transpose(bank[:, u, i * P : (i + 1) * P], words[:, u, :], identity[:])
             grouped = work.tile([P, GROUP * P, PACK], BF16, align_bytes=64)
-            nc.scalar.activation(
-                out=grouped[:].rearrange("p r (u e) -> p r u e", e=2),
-                in_=bank[:].bitcast(BF16).rearrange("p u (r e) -> p r u e", e=2),
-                func=ACT.Copy,
-                scale=sign[:, 0:1],
-            )
+            nc.scalar.copy(out=grouped[:].bitcast(F32), in_=bank[:].rearrange("p u r -> p r u"))
+            return grouped
 
+        def quantise(grouped):
             dz_codes = work.tile([P, GROUP * P], U32, align_bytes=64)
             dz_scales = work.tile([P, GROUP * P], U8, align_bytes=64)
             nc.vector.quantize_mx(
@@ -109,25 +106,57 @@ def tile_middlelayer_t_v_kernel(tc, in_data, W, bias, z, grad_out, out):
                 scales=dz_scales[:],
                 in_=grouped[:].rearrange("p r t -> p (r t)"),
             )
+            return dz_codes, dz_scales
 
-            stage = stages[g % 3]
+        def multiply(g, dz_codes, dz_scales):
+            left = None
             for i in range(GROUP):
                 tokens = slice(i * P, (i + 1) * P)
-                acc = psum_mm.tile([P, FEATURES], F32)
-                nc.tensor.matmul_mx(
-                    out=acc[:],
-                    lhsT=dz_codes[:, tokens].bitcast(E5M2_X4),
-                    lhsT_scale=dz_scales[:, tokens],
-                    rhs=w_codes[:].bitcast(E4M3_X4),
-                    rhs_scale=w_scales[:],
-                    start=True,
-                    stop=True,
-                )
-                nc.scalar.copy(out=stage[:, 1, i * FEATURES : (i + 1) * FEATURES], in_=acc[:])
+                for h in range(OUT_COLS // BANK):
+                    cols = slice(h * BANK, (h + 1) * BANK)
+                    acc = psum_mm.tile([P, BANK], F32)
+                    nc.tensor.matmul_mx(
+                        out=acc[:],
+                        lhsT=dz_codes[:, tokens].bitcast(E5M2_X4),
+                        lhsT_scale=dz_scales[:, tokens],
+                        rhs=w_codes[:, cols].bitcast(E4M3_X4),
+                        rhs_scale=w_scales[:, cols],
+                        start=True,
+                        stop=True,
+                    )
+                    if i == GROUP - 1 and h == 1:
+                        left = acc
+                    else:
+                        nc.scalar.copy(out=out_sb[:, g * GROUP + i, cols], in_=acc[:])
+            return left
 
-            out_group = stores.tile([P, GROUP * FEATURES, 2], F32)
-            nc.vector.tensor_copy(out=out_group[:], in_=stage[:].rearrange("p e m -> p m e"))
-            nc.sync.dma_start(
-                out=out_view[:, tiles, :],
-                in_=out_group[:].rearrange("p (i n) e -> p i (n e)", i=GROUP),
-            )
+        store_ends = []
+        stored = 0
+        while stored < GROUPS:
+            stored += 1
+            store_ends.append(stored)
+
+        def finish(g, left):
+            nc.vector.tensor_copy(out=out_sb[:, g * GROUP + GROUP - 1, BANK:OUT_COLS], in_=left[:])
+            if g + 1 in store_ends:
+                n = store_ends.index(g + 1)
+                first = store_ends[n - 1] if n > 0 else 0
+                tiles = slice(first * GROUP, (g + 1) * GROUP)
+                nc.sync.dma_start(out=out_view[:, tiles, :], in_=out_sb[:, tiles, :])
+
+        grouped_of = {}
+        left_of = {}
+        for s in range(GROUPS + 2):
+            if s < GROUPS:
+                grouped_of[s] = flip(mask(s))
+            if s == 0:
+                nc.vector.quantize_mx(
+                    out=w_codes[:].bitcast(E4M3_X4),
+                    scales=w_scales[:],
+                    in_=w_grouped[:].rearrange("p n j -> p (n j)"),
+                )
+            if 1 <= s <= GROUPS:
+                codes, scales = quantise(grouped_of[s - 1])
+                left_of[s - 1] = multiply(s - 1, codes, scales)
+            if s >= 2:
+                finish(s - 2, left_of[s - 2])

@@ -24,6 +24,7 @@ TILES = TOKENS // P
 GROUP = 2
 GROUPS = TILES // GROUP
 LOAD_MAX = 8
+STORE_MAX = 3
 
 FLOPS = 2 * TOKENS * HIDDEN * FEATURES
 BYTES = TOKENS * HIDDEN * 4 + TOKENS * HALF * 2 + HIDDEN * FEATURES * 2 + TOKENS * 2 * FEATURES * 4
@@ -133,7 +134,7 @@ def tile_middlelayer_t_v_kernel(tc, in_data, W, bias, z, grad_out, out):
         store_ends = []
         stored = 0
         while stored < GROUPS:
-            stored += 1
+            stored += min(STORE_MAX, (GROUPS - stored + 1) // 2)
             store_ends.append(stored)
 
         def finish(g, left):

@@ -23,7 +23,7 @@ BANK = 512
 TILES = TOKENS // P
 GROUP = 2
 GROUPS = TILES // GROUP
-LOAD_MAX = 8
+LOAD_STEP = 4
 STORE_MAX = 3
 
 FLOPS = 2 * TOKENS * HIDDEN * FEATURES
@@ -49,8 +49,9 @@ def tile_middlelayer_t_v_kernel(tc, in_data, W, bias, z, grad_out, out):
         g_sb = keep.tile([P, TILES, HIDDEN], BF16)
         out_sb = keep.tile([P, TILES, OUT_COLS], F32)
         loaded = 0
+        count = 0
         while loaded < TILES:
-            count = min(max(loaded, GROUP), LOAD_MAX)
+            count += LOAD_STEP
             tiles = slice(loaded, loaded + count)
             nc.sync.dma_start(out=z_sb[:, tiles, :], in_=z_view[:, tiles, :])
             nc.sync.dma_start(out=g_sb[:, tiles, :], in_=g_view[:, tiles, :])

@@ -23,8 +23,8 @@ BANK = 512
 TILES = TOKENS // P
 GROUP = 2
 GROUPS = TILES // GROUP
-LOAD_STEP = 4
-STORE_MAX = 3
+LOAD_TILES = 8
+STORE_GROUPS = 2
 
 FLOPS = 2 * TOKENS * HIDDEN * FEATURES
 BYTES = TOKENS * HIDDEN * 4 + TOKENS * HALF * 2 + HIDDEN * FEATURES * 2 + TOKENS * 2 * FEATURES * 4
@@ -49,9 +49,8 @@ def tile_middlelayer_t_v_kernel(tc, in_data, W, bias, z, grad_out, out):
         g_sb = keep.tile([P, TILES, HIDDEN], BF16)
         out_sb = keep.tile([P, TILES, OUT_COLS], F32)
         loaded = 0
-        count = 0
         while loaded < TILES:
-            count += LOAD_STEP
+            count = LOAD_TILES
             tiles = slice(loaded, loaded + count)
             nc.sync.dma_start(out=z_sb[:, tiles, :], in_=z_view[:, tiles, :])
             nc.sync.dma_start(out=g_sb[:, tiles, :], in_=g_view[:, tiles, :])
@@ -135,7 +134,7 @@ def tile_middlelayer_t_v_kernel(tc, in_data, W, bias, z, grad_out, out):
         store_ends = []
         stored = 0
         while stored < GROUPS:
-            stored += min(STORE_MAX, (GROUPS - stored + 1) // 2)
+            stored += STORE_GROUPS
             store_ends.append(stored)
 
         def finish(g, left):

from contextlib import ExitStack

import concourse.masks as masks
import concourse.mybir as mybir

F32 = mybir.dt.float32
BF16 = mybir.dt.bfloat16
U32 = mybir.dt.uint32
U8 = mybir.dt.uint8
E4M3_X4 = mybir.dt.float8_e4m3fn_x4
E5M2_X4 = mybir.dt.float8_e5m2_x4
ALU = mybir.AluOpType
ACT = mybir.ActivationFunctionType

P = 128
PACK = 4
TOKENS = 3072
HIDDEN = P * PACK
HALF = HIDDEN // 2
FEATURES = 512
OUT_COLS = 2 * FEATURES
BANK = 512
TILES = TOKENS // P
GROUP = 2
GROUPS = TILES // GROUP
LOAD_TILES = 8
STORE_GROUPS = 2

FLOPS = 2 * TOKENS * HIDDEN * FEATURES
BYTES = TOKENS * HIDDEN * 4 + TOKENS * HALF * 2 + HIDDEN * FEATURES * 2 + TOKENS * 2 * FEATURES * 4


def tile_middlelayer_t_v_kernel(tc, in_data, W, bias, z, grad_out, out):
    nc = tc.nc
    z_view = z.rearrange("(p t) k -> p t k", t=TILES)
    g_view = grad_out.rearrange("(p t) k o -> p t (k o)", t=TILES)
    out_view = out.rearrange("(p t) n -> p t n", t=TILES)

    with ExitStack() as ctx:
        keep = ctx.enter_context(tc.tile_pool(name="keep", bufs=1))
        work = ctx.enter_context(tc.tile_pool(name="work", bufs=3))
        psum_t = ctx.enter_context(tc.psum_pool(name="psum_t", bufs=2))
        psum_mm = ctx.enter_context(tc.psum_pool(name="psum_mm", bufs=6))
        ctx.enter_context(tc.manual_schedule())

        w_rows = keep.tile([P, PACK, FEATURES], BF16)
        nc.sync.dma_start(out=w_rows[:], in_=W.rearrange("(p j) n -> p j n", j=PACK))
        z_sb = keep.tile([P, TILES, HIDDEN], F32)
        g_sb = keep.tile([P, TILES, HIDDEN], BF16)
        out_sb = keep.tile([P, TILES, OUT_COLS], F32)
        loaded = 0
        while loaded < TILES:
            count = LOAD_TILES
            tiles = slice(loaded, loaded + count)
            nc.sync.dma_start(out=z_sb[:, tiles, :], in_=z_view[:, tiles, :])
            nc.sync.dma_start(out=g_sb[:, tiles, :], in_=g_view[:, tiles, :])
            loaded += count

        identity = keep.tile([P, P], F32)
        masks.make_identity(nc, identity[:])
        sign = keep.tile([P, 1], F32)
        nc.vector.memset(sign[0 : P // 2, :], 1.0)
        nc.vector.memset(sign[P // 2 : P, :], -1.0)

        w_grouped = keep.tile([P, OUT_COLS, PACK], BF16, align_bytes=64)
        w_pairs = w_grouped[:].rearrange("p (n e) j -> p n e j", e=2)
        nc.vector.memset(w_pairs[:, :, 0, :], 0.0)
        nc.scalar.activation(
            out=w_pairs[:, :, 1, :],
            in_=w_rows[:].rearrange("p j n -> p n j"),
            func=ACT.Copy,
            scale=sign[:, 0:1],
        )
        w_codes = keep.tile([P, OUT_COLS], U32, align_bytes=64)
        w_scales = keep.tile([P, OUT_COLS], U8, align_bytes=64)

        def mask(g):
            masked = work.tile([P, GROUP, HIDDEN], BF16)
            for i in range(GROUP):
                t = g * GROUP + i
                g_even = g_sb[:, t, :].rearrange("p (j s) -> p s j", s=2)[:, 0:1, :]
                nc.vector.scalar_tensor_tensor(
                    out=masked[:, i, :].rearrange("p (h j) -> p h j", h=2),
                    in0=z_sb[:, t, :].rearrange("p (h j) -> p h j", h=2),
                    scalar=0.0,
                    in1=g_even.to_broadcast([P, 2, HALF]),
                    op0=ALU.is_gt,
                    op1=ALU.mult,
                )
            return masked

        def flip(masked):
            bank = psum_t.tile([P, 2, GROUP * P], F32)
            for i in range(GROUP):
                words = masked[:, i, :].bitcast(F32).rearrange("p (q u) -> p u q", u=2)
                for u in range(2):
                    nc.tensor.transpose(bank[:, u, i * P : (i + 1) * P], words[:, u, :], identity[:])
            grouped = work.tile([P, GROUP * P, PACK], BF16, align_bytes=64)
            nc.scalar.copy(out=grouped[:].bitcast(F32), in_=bank[:].rearrange("p u r -> p r u"))
            return grouped

        def quantise(grouped):
            dz_codes = work.tile([P, GROUP * P], U32, align_bytes=64)
            dz_scales = work.tile([P, GROUP * P], U8, align_bytes=64)
            nc.vector.quantize_mx(
                out=dz_codes[:].bitcast(E5M2_X4),
                scales=dz_scales[:],
                in_=grouped[:].rearrange("p r t -> p (r t)"),
            )
            return dz_codes, dz_scales

        def multiply(g, dz_codes, dz_scales):
            left = None
            for i in range(GROUP):
                tokens = slice(i * P, (i + 1) * P)
                for h in range(OUT_COLS // BANK):
                    cols = slice(h * BANK, (h + 1) * BANK)
                    acc = psum_mm.tile([P, BANK], F32)
                    nc.tensor.matmul_mx(
                        out=acc[:],
                        lhsT=dz_codes[:, tokens].bitcast(E5M2_X4),
                        lhsT_scale=dz_scales[:, tokens],
                        rhs=w_codes[:, cols].bitcast(E4M3_X4),
                        rhs_scale=w_scales[:, cols],
                        start=True,
                        stop=True,
                    )
                    if i == GROUP - 1 and h == 1:
                        left = acc
                    else:
                        nc.scalar.copy(out=out_sb[:, g * GROUP + i, cols], in_=acc[:])
            return left

        store_ends = []
        stored = 0
        while stored < GROUPS:
            stored += STORE_GROUPS
            store_ends.append(stored)

        def finish(g, left):
            nc.vector.tensor_copy(out=out_sb[:, g * GROUP + GROUP - 1, BANK:OUT_COLS], in_=left[:])
            if g + 1 in store_ends:
                n = store_ends.index(g + 1)
                first = store_ends[n - 1] if n > 0 else 0
                tiles = slice(first * GROUP, (g + 1) * GROUP)
                nc.sync.dma_start(out=out_view[:, tiles, :], in_=out_sb[:, tiles, :])

        grouped_of = {}
        left_of = {}
        for s in range(GROUPS + 2):
            if s < GROUPS:
                grouped_of[s] = flip(mask(s))
            if s == 0:
                nc.vector.quantize_mx(
                    out=w_codes[:].bitcast(E4M3_X4),
                    scales=w_scales[:],
                    in_=w_grouped[:].rearrange("p n j -> p (n j)"),
                )
            if 1 <= s <= GROUPS:
                codes, scales = quantise(grouped_of[s - 1])
                left_of[s - 1] = multiply(s - 1, codes, scales)
            if s >= 2:
                finish(s - 2, left_of[s - 2])
